import numpy as np
import ml_dtypes


def mxq(x, axis, fmt="e4m3"):
    dtype, down = {"e4m3": (ml_dtypes.float8_e4m3fn, 7), "e5m2": (ml_dtypes.float8_e5m2, 14)}[fmt]
    v = np.moveaxis(np.asarray(x, np.float32).astype(ml_dtypes.bfloat16).astype(np.float64), axis, -1)
    blocks = v.reshape(v.shape[:-1] + (-1, 32))
    amax = np.abs(blocks).max(-1, keepdims=True)
    byte = np.maximum(np.where(amax > 0, np.frexp(amax)[1] - 1 + 127, 0) - down, 1)
    scale = np.exp2(byte - 127.0)
    codes = (blocks / scale).astype(np.float32).astype(dtype).astype(np.float64)
    return np.moveaxis((codes * scale).reshape(v.shape), -1, axis)


WIDE = False


def mx_kscale(k):
    if not WIDE:
        return np.ones(k)
    levels = np.array([10, -10, 5, -5, 0])
    a = np.random.permutation(np.resize(levels, k // 512 * 4)).reshape(k // 512, 4)
    idx = np.arange(k)
    return np.exp2(a[idx // 512, idx % 128 // 32])


BF16 = ml_dtypes.bfloat16


def bf(x):
    return np.asarray(x, np.float32).astype(BF16)


def f64(x):
    return np.asarray(x).astype(np.float64)


B, C, H, W = 3, 512, 64, 64
BETA_MIN = 1e-06
REPARAM_OFFSET = 2.0 ** (-18)
PEDESTAL = REPARAM_OFFSET ** 2
BETA_BOUND = (BETA_MIN + PEDESTAL) ** 0.5
GAMMA_BOUND = REPARAM_OFFSET


def setup_inputs():
    t = np.exp2(np.round(np.log2(mx_kscale(C)) / 2))
    amp = np.exp(0.5 * np.random.standard_normal((B, 1, H, W)))
    return {"inputs": bf(np.random.standard_normal((B, C, H, W)) * amp * t[None, :, None, None]),
            "beta": bf((0.5 + np.random.standard_normal(C)) * t),
            "gamma": bf(np.random.standard_normal((C, C)) * 1.4 / np.sqrt(C) * t[:, None] / t[None, :])}


def reference(inputs, beta, gamma):
    x = f64(inputs)
    beta_c = np.maximum(f64(beta), BETA_BOUND) ** 2 - PEDESTAL
    gamma_c = np.maximum(f64(gamma), GAMMA_BOUND) ** 2 - PEDESTAL
    x2 = (x ** 2).reshape(B, C, H * W)
    norm = (mxq(gamma_c, 1, "e4m3") @ mxq(x2, 1, "e4m3")).reshape(B, C, H, W)
    norm = np.sqrt(norm + beta_c[None, :, None, None])
    return x / norm

@@ -1,0 +1,151 @@
+from contextlib import ExitStack
+
+import concourse.bass as bass
+import concourse.mybir as mybir
+import concourse.tile as tile
+from concourse.masks import make_identity
+
+FLOPS = 2 * 512 * 512 * 3 * 4096
+
+BF16 = mybir.dt.bfloat16
+F32 = mybir.dt.float32
+U32 = mybir.dt.uint32
+U8 = mybir.dt.uint8
+FP8X4 = mybir.dt.float8_e4m3fn_x4
+ALU = mybir.AluOpType
+ACT = mybir.ActivationFunctionType
+
+P = 128
+PACK = 4
+BATCH = 3
+PIX = 4096
+CH = 512
+N_CHUNKS = BATCH * PIX // CH
+RES_CH = 2
+LEAD = 4
+S_COLS = 320
+
+REPARAM = 2.0 ** (-18)
+PEDESTAL = REPARAM * REPARAM
+BETA_BOUND = (1e-06 + PEDESTAL) ** 0.5
+
+PIECES = [(0, 0, 512), (0, 512, 512), (0, 1024, 1024), (0, 2048, 2048),
+          (1, 0, 2048), (1, 2048, 2048), (2, 0, 2048), (2, 2048, 2048)]
+
+
+def tile_gdn_t_kernel(tc, inputs, beta, gamma, out):
+    nc = tc.nc
+    x_dram = inputs.rearrange("b (p j) h w -> b p j (h w)", j=PACK)
+    o_dram = out.rearrange("b (p j) h w -> b p j (h w)", j=PACK)
+
+    with ExitStack() as ctx:
+        const = ctx.enter_context(tc.tile_pool(name="const", bufs=1))
+        xpool = ctx.enter_context(tc.tile_pool(name="xpool", bufs=1))
+        gpool = ctx.enter_context(tc.tile_pool(name="gpool", bufs=3))
+        cpool = ctx.enter_context(tc.tile_pool(name="cpool", bufs=LEAD + 2))
+        rpool = ctx.enter_context(tc.tile_pool(name="rpool", bufs=5))
+        psum = ctx.enter_context(tc.psum_pool(name="psum", bufs=8))
+
+        warm = const.tile([P, 1], F32, name="warm")
+        nc.vector.memset(warm[:], 1.0)
+        nc.scalar.activation(out=warm[:], in_=warm[:], func=ACT.Abs_reciprocal_sqrt)
+
+        ident = const.tile([P, P], BF16, name="ident")
+        make_identity(nc, ident[:])
+
+        g_raw = const.tile([P, PACK, 512], BF16, name="g_raw")
+        nc.sync.dma_start(out=g_raw[:], in_=gamma.rearrange("(m j) c -> m j c", j=PACK))
+        xt = []
+        for n, (b, w0, width) in enumerate(PIECES):
+            t = xpool.tile([P, PACK, width], BF16, name="x%d" % n)
+            nc.sync.dma_start(out=t[:], in_=x_dram[b, :, :, w0:w0 + width])
+            xt.append(t)
+            if n == 0:
+                b_raw = const.tile([P, PACK], BF16, name="b_raw")
+                nc.sync.dma_start(out=b_raw[:], in_=beta.rearrange("(p j) -> p j", j=PACK))
+
+        def x_chunk(i):
+            b, w0 = divmod(i * CH, PIX)
+            for n, (pb, pw, width) in enumerate(PIECES):
+                if pb == b and pw <= w0 < pw + width:
+                    return xt[n][:, :, w0 - pw:w0 - pw + CH]
+            raise ValueError("no piece")
+
+        g_u = const.tile([P, PACK, 512], F32, name="g_u")
+        nc.vector.tensor_scalar(out=g_u[:], in0=g_raw[:], scalar1=REPARAM, scalar2=-REPARAM,
+                                op0=ALU.max, op1=ALU.add)
+        g_c = const.tile([P, PACK, PACK, P], BF16, name="g_c")
+        for j in range(PACK):
+            u_v = g_u[:, j, :].rearrange("m (p t) -> m t p", t=PACK)
+            nc.vector.scalar_tensor_tensor(out=g_c[:, j, :, :], in0=u_v, scalar=2.0 * REPARAM,
+                                           in1=u_v, op0=ALU.add, op1=ALU.mult)
+        g_grp = const.tile([P, 512, PACK], BF16, name="g_grp", align_bytes=64)
+        for h in range(2):
+            tp = psum.tile([P, 8, P], BF16, name="tp", tag="acc")
+            for jj in range(2):
+                for t in range(PACK):
+                    nc.tensor.transpose(tp[:, jj * PACK + t, :], g_c[:, 2 * h + jj, t, :], ident[:])
+            dst = g_grp[:, 256 * h:256 * h + 256, :].rearrange("p (jj m) t -> p jj m t", jj=2)
+            src = tp[:].rearrange("p (jj t) m -> p jj m t", t=PACK)
+            if h == 0:
+                nc.vector.tensor_copy(out=dst, in_=src)
+            else:
+                nc.scalar.copy(out=dst, in_=src)
+        g_codes = const.tile([P, 512], U32, name="g_codes", align_bytes=64)
+        g_scales = const.tile([P, 512], U8, name="g_scales", align_bytes=64)
+        nc.vector.quantize_mx(out=g_codes[:].bitcast(FP8X4), scales=g_scales[:],
+                              in_=g_grp[:].rearrange("p w t -> p (w t)"))
+
+        b_t = const.tile([P, PACK], F32, name="b_t")
+        nc.vector.tensor_scalar_max(out=b_t[:], in0=b_raw[:], scalar1=BETA_BOUND)
+        b_c = const.tile([P, PACK], F32, name="b_c")
+        nc.vector.tensor_tensor(out=b_c[:], in0=b_t[:], in1=b_t[:], op=ALU.mult)
+        nc.vector.tensor_scalar_add(out=b_c[:], in0=b_c[:], scalar1=-PEDESTAL)
+
+        quantised = {}
+        results = {}
+
+        def front(i):
+            sc = CH if i < LEAD else S_COLS
+            xs = x_chunk(i)
+            grp = gpool.tile([P, CH, PACK], BF16, name="grp", align_bytes=64)
+            nc.scalar.activation(
+                out=grp[:, 0:sc, :].rearrange("p (c i) t -> p c t i", i=4),
+                in_=xs[:, :, 0:sc].rearrange("p t (c i) -> p c t i", i=4),
+                func=ACT.Square)
+            if sc < CH:
+                xv = xs[:, :, sc:CH].rearrange("p t w -> p w t")
+                nc.vector.tensor_tensor(out=grp[:, sc:CH, :], in0=xv, in1=xv, op=ALU.mult)
+            codes = cpool.tile([P, CH], U32, name="codes", align_bytes=64)
+            scales = cpool.tile([P, CH], U8, name="scales", align_bytes=64)
+            nc.vector.quantize_mx(out=codes[:].bitcast(FP8X4), scales=scales[:],
+                                  in_=grp[:].rearrange("p w t -> p (w t)"))
+            quantised[i] = (codes, scales)
+
+        def back(i):
+            codes, scales = quantised[i]
+            k = i % RES_CH
+            if k == 0:
+                res_new = rpool.tile([P, PACK, RES_CH * CH], F32, name="res")
+                results[i // RES_CH] = res_new
+            res = results[i // RES_CH]
+            rs = res[:, :, k * CH:(k + 1) * CH]
+            for j in range(PACK):
+                acc = psum.tile([P, CH], F32, name="acc", tag="acc")
+                nc.tensor.matmul_mx(out=acc[:],
+                                    lhsT=g_codes[:, P * j:P * j + P].bitcast(FP8X4),
+                                    lhsT_scale=g_scales[:, P * j:P * j + P],
+                                    rhs=codes[:].bitcast(FP8X4), rhs_scale=scales[:],
+                                    start=True, stop=True)
+                nc.scalar.activation(out=res[:, j, k * CH:(k + 1) * CH], in_=acc[:],
+                                     func=ACT.Abs_reciprocal_sqrt, bias=b_c[:, j:j + 1], scale=1.0)
+            nc.vector.tensor_tensor(out=rs, in0=x_chunk(i), in1=rs, op=ALU.mult)
+            if k == RES_CH - 1:
+                b, w1 = divmod((i + 1) * CH - RES_CH * CH, PIX)
+                nc.sync.dma_start(out=o_dram[b, :, :, w1:w1 + RES_CH * CH], in_=res[:])
+
+        for r in range(-LEAD, N_CHUNKS):
+            if r + LEAD < N_CHUNKS:
+                front(r + LEAD)
+            if r >= 0:
+                back(r)

@@ -1,8 +1,6 @@
 from contextlib import ExitStack
 
-import concourse.bass as bass
 import concourse.mybir as mybir
-import concourse.tile as tile
 from concourse.masks import make_identity
 
 FLOPS = 2 * 512 * 512 * 3 * 4096
@@ -21,15 +19,18 @@ BATCH = 3
 PIX = 4096
 CH = 512
 N_CHUNKS = BATCH * PIX // CH
-RES_CH = 2
-LEAD = 4
-S_COLS = 320
+AHEAD = 5
+S_ALONE = 3
+S_COLS = 312
+SPREAD = 22
+PAIRS_TO = 20
+PINNED = True
 
 REPARAM = 2.0 ** (-18)
 PEDESTAL = REPARAM * REPARAM
 BETA_BOUND = (1e-06 + PEDESTAL) ** 0.5
 
-PIECES = [(0, 0, 512), (0, 512, 512), (0, 1024, 1024), (0, 2048, 2048),
+PIECES = [(0, 0, 256), (0, 256, 256), (0, 512, 512), (0, 1024, 1024), (0, 2048, 1024), (0, 3072, 1024),
           (1, 0, 2048), (1, 2048, 2048), (2, 0, 2048), (2, 2048, 2048)]
 
 
@@ -41,10 +42,13 @@ def tile_gdn_t_kernel(tc, inputs, beta, gamma, out):
     with ExitStack() as ctx:
         const = ctx.enter_context(tc.tile_pool(name="const", bufs=1))
         xpool = ctx.enter_context(tc.tile_pool(name="xpool", bufs=1))
-        gpool = ctx.enter_context(tc.tile_pool(name="gpool", bufs=3))
-        cpool = ctx.enter_context(tc.tile_pool(name="cpool", bufs=LEAD + 2))
-        rpool = ctx.enter_context(tc.tile_pool(name="rpool", bufs=5))
+        gpool = ctx.enter_context(tc.tile_pool(name="gpool", bufs=4))
+        spool = ctx.enter_context(tc.tile_pool(name="spool", bufs=2))
+        cpool = ctx.enter_context(tc.tile_pool(name="cpool", bufs=AHEAD + 3))
+        rpool = ctx.enter_context(tc.tile_pool(name="rpool", bufs=4))
         psum = ctx.enter_context(tc.psum_pool(name="psum", bufs=8))
+        if PINNED:
+            ctx.enter_context(tc.manual_schedule())
 
         warm = const.tile([P, 1], F32, name="warm")
         nc.vector.memset(warm[:], 1.0)
@@ -54,82 +58,115 @@ def tile_gdn_t_kernel(tc, inputs, beta, gamma, out):
         make_identity(nc, ident[:])
 
         g_raw = const.tile([P, PACK, 512], BF16, name="g_raw")
-        nc.sync.dma_start(out=g_raw[:], in_=gamma.rearrange("(m j) c -> m j c", j=PACK))
+        b_raw = const.tile([P, PACK], BF16, name="b_raw")
         xt = []
         for n, (b, w0, width) in enumerate(PIECES):
             t = xpool.tile([P, PACK, width], BF16, name="x%d" % n)
             nc.sync.dma_start(out=t[:], in_=x_dram[b, :, :, w0:w0 + width])
             xt.append(t)
             if n == 0:
-                b_raw = const.tile([P, PACK], BF16, name="b_raw")
+                nc.sync.dma_start(out=g_raw[:], in_=gamma.rearrange("(m j) c -> m j c", j=PACK))
+            if n == 2:
                 nc.sync.dma_start(out=b_raw[:], in_=beta.rearrange("(p j) -> p j", j=PACK))
 
-        def x_chunk(i):
+        def x_parts(i):
             b, w0 = divmod(i * CH, PIX)
-            for n, (pb, pw, width) in enumerate(PIECES):
-                if pb == b and pw <= w0 < pw + width:
-                    return xt[n][:, :, w0 - pw:w0 - pw + CH]
-            raise ValueError("no piece")
+            parts = []
+            for k, (pb, pw, width) in enumerate(PIECES):
+                lo = max(pw, w0)
+                hi = min(pw + width, w0 + CH)
+                if pb == b and lo < hi:
+                    parts.append((lo - w0, hi - lo, xt[k][:, :, lo - pw:hi - pw]))
+            return parts
 
-        g_u = const.tile([P, PACK, 512], F32, name="g_u")
-        nc.vector.tensor_scalar(out=g_u[:], in0=g_raw[:], scalar1=REPARAM, scalar2=-REPARAM,
-                                op0=ALU.max, op1=ALU.add)
-        g_c = const.tile([P, PACK, PACK, P], BF16, name="g_c")
-        for j in range(PACK):
-            u_v = g_u[:, j, :].rearrange("m (p t) -> m t p", t=PACK)
-            nc.vector.scalar_tensor_tensor(out=g_c[:, j, :, :], in0=u_v, scalar=2.0 * REPARAM,
-                                           in1=u_v, op0=ALU.add, op1=ALU.mult)
-        g_grp = const.tile([P, 512, PACK], BF16, name="g_grp", align_bytes=64)
-        for h in range(2):
-            tp = psum.tile([P, 8, P], BF16, name="tp", tag="acc")
-            for jj in range(2):
-                for t in range(PACK):
-                    nc.tensor.transpose(tp[:, jj * PACK + t, :], g_c[:, 2 * h + jj, t, :], ident[:])
-            dst = g_grp[:, 256 * h:256 * h + 256, :].rearrange("p (jj m) t -> p jj m t", jj=2)
-            src = tp[:].rearrange("p (jj t) m -> p jj m t", t=PACK)
-            if h == 0:
-                nc.vector.tensor_copy(out=dst, in_=src)
-            else:
-                nc.scalar.copy(out=dst, in_=src)
         g_codes = const.tile([P, 512], U32, name="g_codes", align_bytes=64)
         g_scales = const.tile([P, 512], U8, name="g_scales", align_bytes=64)
-        nc.vector.quantize_mx(out=g_codes[:].bitcast(FP8X4), scales=g_scales[:],
-                              in_=g_grp[:].rearrange("p w t -> p (w t)"))
+        b_c = const.tile([P, PACK], F32, name="b_c")
+        t_banks = []
 
         b_t = const.tile([P, PACK], F32, name="b_t")
-        nc.vector.tensor_scalar_max(out=b_t[:], in0=b_raw[:], scalar1=BETA_BOUND)
-        b_c = const.tile([P, PACK], F32, name="b_c")
-        nc.vector.tensor_tensor(out=b_c[:], in0=b_t[:], in1=b_t[:], op=ALU.mult)
-        nc.vector.tensor_scalar_add(out=b_c[:], in0=b_c[:], scalar1=-PEDESTAL)
+        g_grp = const.tile([P, 512, PACK], BF16, name="g_grp", align_bytes=64)
 
+        def gamma_to_psum():
+            g_u = const.tile([P, PACK, 512], F32, name="g_u")
+            g_c = const.tile([P, PACK, PACK, P], BF16, name="g_c")
+
+            def shifted(j):
+                nc.vector.tensor_scalar(out=g_u[:, j, :], in0=g_raw[:, j, :], scalar1=REPARAM,
+                                        scalar2=-REPARAM, op0=ALU.max, op1=ALU.add)
+
+            def squared_minus(j):
+                u_v = g_u[:, j, :].rearrange("m (p t) -> m t p", t=PACK)
+                nc.vector.scalar_tensor_tensor(out=g_c[:, j, :, :], in0=u_v, scalar=2.0 * REPARAM,
+                                               in1=u_v, op0=ALU.add, op1=ALU.mult)
+
+            shifted(0)
+            for j in range(PACK):
+                if j + 1 < PACK:
+                    shifted(j + 1)
+                squared_minus(j)
+            for h in range(2):
+                tp = psum.tile([P, 8, P], BF16, name="tp", tag="acc")
+                for jj in range(2):
+                    for t in range(PACK):
+                        nc.tensor.transpose(tp[:, jj * PACK + t, :], g_c[:, 2 * h + jj, t, :], ident[:])
+                t_banks.append(tp)
+
+        def gamma_out(h):
+            nc.vector.tensor_copy(
+                out=g_grp[:, 256 * h:256 * h + 256, :].rearrange("p (jj m) t -> p jj m t", jj=2),
+                in_=t_banks[h][:].rearrange("p (jj t) m -> p jj m t", t=PACK))
+
+        def gamma_quantise():
+            nc.vector.quantize_mx(out=g_codes[:].bitcast(FP8X4), scales=g_scales[:],
+                                  in_=g_grp[:].rearrange("p w t -> p (w t)"))
+
+        def beta_step(n):
+            if n == 0:
+                nc.vector.tensor_scalar_max(out=b_t[:], in0=b_raw[:], scalar1=BETA_BOUND)
+            elif n == 1:
+                nc.vector.tensor_tensor(out=b_t[:], in0=b_t[:], in1=b_t[:], op=ALU.mult)
+            else:
+                nc.vector.tensor_scalar_add(out=b_c[:], in0=b_t[:], scalar1=-PEDESTAL)
+
+        halves = {}
+        grouped = {}
         quantised = {}
         results = {}
+        banks = {}
 
-        def front(i):
-            sc = CH if i < LEAD else S_COLS
-            xs = x_chunk(i)
+        def square_a(i):
             grp = gpool.tile([P, CH, PACK], BF16, name="grp", align_bytes=64)
-            nc.scalar.activation(
-                out=grp[:, 0:sc, :].rearrange("p (c i) t -> p c t i", i=4),
-                in_=xs[:, :, 0:sc].rearrange("p t (c i) -> p c t i", i=4),
-                func=ACT.Square)
-            if sc < CH:
-                xv = xs[:, :, sc:CH].rearrange("p t w -> p w t")
-                nc.vector.tensor_tensor(out=grp[:, sc:CH, :], in0=xv, in1=xv, op=ALU.mult)
+            grouped[i] = grp
+            halves[i] = []
+            sc = CH if i < S_ALONE else S_COLS
+            for c0, n, xs in x_parts(i):
+                ns = max(0, min(n, sc - c0))
+                if ns > 0:
+                    nc.scalar.activation(
+                        out=grp[:, c0:c0 + ns, :].rearrange("p (c i) t -> p c t i", i=4),
+                        in_=xs[:, :, 0:ns].rearrange("p t (c i) -> p c t i", i=4),
+                        func=ACT.Square)
+                if ns < n:
+                    sq = spool.tile([P, PACK, n - ns], BF16, name="sq")
+                    nc.vector.tensor_tensor(out=sq[:], in0=xs[:, :, ns:n], in1=xs[:, :, ns:n], op=ALU.mult)
+                    halves[i].append((c0 + ns, c0 + n, sq))
+
+        def square_b(i):
+            for lo, hi, sq in halves[i]:
+                nc.vector.tensor_copy(
+                    out=grouped[i][:, lo:hi, :].rearrange("p (c i) t -> p c t i", i=4),
+                    in_=sq[:].rearrange("p t (c i) -> p c t i", i=4))
+
+        def quantise(i):
             codes = cpool.tile([P, CH], U32, name="codes", align_bytes=64)
             scales = cpool.tile([P, CH], U8, name="scales", align_bytes=64)
             nc.vector.quantize_mx(out=codes[:].bitcast(FP8X4), scales=scales[:],
-                                  in_=grp[:].rearrange("p w t -> p (w t)"))
+                                  in_=grouped[i][:].rearrange("p w t -> p (w t)"))
             quantised[i] = (codes, scales)
 
-        def back(i):
+        def multiply(i):
             codes, scales = quantised[i]
-            k = i % RES_CH
-            if k == 0:
-                res_new = rpool.tile([P, PACK, RES_CH * CH], F32, name="res")
-                results[i // RES_CH] = res_new
-            res = results[i // RES_CH]
-            rs = res[:, :, k * CH:(k + 1) * CH]
             for j in range(PACK):
                 acc = psum.tile([P, CH], F32, name="acc", tag="acc")
                 nc.tensor.matmul_mx(out=acc[:],
@@ -137,15 +174,76 @@ def tile_gdn_t_kernel(tc, inputs, beta, gamma, out):
                                     lhsT_scale=g_scales[:, P * j:P * j + P],
                                     rhs=codes[:].bitcast(FP8X4), rhs_scale=scales[:],
                                     start=True, stop=True)
-                nc.scalar.activation(out=res[:, j, k * CH:(k + 1) * CH], in_=acc[:],
-                                     func=ACT.Abs_reciprocal_sqrt, bias=b_c[:, j:j + 1], scale=1.0)
-            nc.vector.tensor_tensor(out=rs, in0=x_chunk(i), in1=rs, op=ALU.mult)
-            if k == RES_CH - 1:
-                b, w1 = divmod((i + 1) * CH - RES_CH * CH, PIX)
-                nc.sync.dma_start(out=o_dram[b, :, :, w1:w1 + RES_CH * CH], in_=res[:])
+                banks[(i, j)] = acc
 
-        for r in range(-LEAD, N_CHUNKS):
-            if r + LEAD < N_CHUNKS:
-                front(r + LEAD)
-            if r >= 0:
-                back(r)
+        def res_view(i):
+            return results[i // 2][:, :, (i % 2) * CH:(i % 2 + 1) * CH]
+
+        def rsqrt(i, j):
+            if i % 2 == 0 and j == 0:
+                res_new = rpool.tile([P, PACK, 2 * CH], F32, name="res")
+                results[i // 2] = res_new
+            nc.scalar.activation(out=res_view(i)[:, j, :], in_=banks[(i, j)][:],
+                                 func=ACT.Abs_reciprocal_sqrt, bias=b_c[:, j:j + 1], scale=1.0)
+
+        def scale_x(i, j0, j1):
+            for c0, n, xs in x_parts(i):
+                rs = res_view(i)[:, j0:j1, c0:c0 + n]
+                nc.vector.tensor_tensor(out=rs, in0=xs[:, j0:j1, :], in1=rs, op=ALU.mult)
+
+        def store(i0, i1, j0, j1):
+            b, w0 = divmod(i0 * CH, PIX)
+            n = (i1 - i0) * CH
+            k0 = (i0 % 2) * CH
+            nc.sync.dma_start(out=o_dram[b, :, j0:j1, w0:w0 + n],
+                              in_=results[i0 // 2][:, j0:j1, k0:k0 + n])
+
+        def store_chunk(i):
+            if i >= PAIRS_TO:
+                store(i, i + 1, 0, PACK)
+            elif i % 2 == 1:
+                store(i - 1, i + 1, 0, PACK)
+
+        square_a(0)
+        gamma_to_psum()
+        beta_step(0)
+        quantise(0)
+        beta_step(1)
+        gamma_out(0)
+        beta_step(2)
+        gamma_out(1)
+        square_a(1)
+        square_a(2)
+        quantise(1)
+        gamma_quantise()
+        for i in range(3, AHEAD):
+            square_a(i)
+            quantise(i - 1)
+            square_b(i)
+        squared = AHEAD
+        for r in range(N_CHUNKS):
+            multiply(r)
+            if r >= 1:
+                scale_x(r - 1, 2, PACK)
+                store_chunk(r - 1)
+            want = min(N_CHUNKS, AHEAD + ((r + 1) * (N_CHUNKS - AHEAD) + SPREAD - 1) // SPREAD)
+            fresh = squared < want
+            if fresh:
+                square_a(squared)
+            if (squared - 1) not in quantised:
+                quantise(squared - 1)
+            if fresh:
+                square_b(squared)
+                squared += 1
+            if r < N_CHUNKS - 1:
+                rsqrt(r, 0)
+                rsqrt(r, 1)
+                scale_x(r, 0, 2)
+                rsqrt(r, 2)
+                rsqrt(r, 3)
+            else:
+                for j in range(PACK):
+                    rsqrt(r, j)
+                    scale_x(r, j, j + 1)
+                    if j >= 1:
+                        store(r, r + 1, 0 if j == 1 else j, j + 1)

@@ -22,8 +22,11 @@ N_CHUNKS = BATCH * PIX // CH
 AHEAD = 5
 S_ALONE = 3
 S_COLS = 312
+S_COLS_D = 256
+D_FIRST = 1
+D_LAST = 18
 SPREAD = 22
-PAIRS_TO = 20
+PAIRS_TO = 0
 PINNED = True
 
 REPARAM = 2.0 ** (-18)
@@ -135,11 +138,11 @@ def tile_gdn_t_kernel(tc, inputs, beta, gamma, out):
         results = {}
         banks = {}
 
-        def square_a(i):
+        def square_a(i, cols):
             grp = gpool.tile([P, CH, PACK], BF16, name="grp", align_bytes=64)
             grouped[i] = grp
             halves[i] = []
-            sc = CH if i < S_ALONE else S_COLS
+            sc = cols
             for c0, n, xs in x_parts(i):
                 ns = max(0, min(n, sc - c0))
                 if ns > 0:
@@ -204,7 +207,27 @@ def tile_gdn_t_kernel(tc, inputs, beta, gamma, out):
             elif i % 2 == 1:
                 store(i - 1, i + 1, 0, PACK)
 
-        square_a(0)
+        x_banks = {}
+
+        def shared(i):
+            return D_FIRST <= i <= D_LAST
+
+        def x_to_psum(i, j):
+            c0, n, xs = x_parts(i)[0]
+            xp = psum.tile([P, CH], F32, name="xp", tag="acc")
+            nc.tensor.matmul(out=xp[:], lhsT=ident[:], rhs=xs[:, j, :], start=True, stop=True)
+            x_banks[(i, j)] = xp
+
+        def scale_from_psum(i, j):
+            rs = res_view(i)[:, j, :]
+            nc.vector.tensor_tensor(out=rs, in0=x_banks[(i, j)][:], in1=rs, op=ALU.mult)
+
+        def scale_on_gpsimd(i, j):
+            c0, n, xs = x_parts(i)[0]
+            rs = res_view(i)[:, j, :]
+            nc.gpsimd.tensor_tensor(out=rs, in0=xs[:, j, :], in1=rs, op=ALU.mult)
+
+        square_a(0, CH)
         gamma_to_psum()
         beta_step(0)
         quantise(0)
@@ -212,24 +235,31 @@ def tile_gdn_t_kernel(tc, inputs, beta, gamma, out):
         gamma_out(0)
         beta_step(2)
         gamma_out(1)
-        square_a(1)
-        square_a(2)
+        square_a(1, CH)
+        square_a(2, CH)
         quantise(1)
         gamma_quantise()
         for i in range(3, AHEAD):
-            square_a(i)
+            square_a(i, S_COLS)
             quantise(i - 1)
             square_b(i)
         squared = AHEAD
         for r in range(N_CHUNKS):
+            c = r - 1
             multiply(r)
-            if r >= 1:
-                scale_x(r - 1, 2, PACK)
-                store_chunk(r - 1)
+            if shared(r):
+                x_to_psum(r, 0)
+                x_to_psum(r, 3)
+            if c >= 0:
+                if shared(c):
+                    scale_x(c, 2, 3)
+                else:
+                    scale_x(c, 2, PACK)
+                    store_chunk(c)
             want = min(N_CHUNKS, AHEAD + ((r + 1) * (N_CHUNKS - AHEAD) + SPREAD - 1) // SPREAD)
             fresh = squared < want
             if fresh:
-                square_a(squared)
+                square_a(squared, S_COLS_D if shared(r) else S_COLS)
             if (squared - 1) not in quantised:
                 quantise(squared - 1)
             if fresh:
@@ -237,8 +267,16 @@ def tile_gdn_t_kernel(tc, inputs, beta, gamma, out):
                 squared += 1
             if r < N_CHUNKS - 1:
                 rsqrt(r, 0)
-                rsqrt(r, 1)
-                scale_x(r, 0, 2)
+                if c >= 0 and shared(c):
+                    scale_from_psum(c, 3)
+                    store_chunk(c)
+                if shared(r):
+                    scale_from_psum(r, 0)
+                    rsqrt(r, 1)
+                    scale_on_gpsimd(r, 1)
+                else:
+                    rsqrt(r, 1)
+                    scale_x(r, 0, 2)
                 rsqrt(r, 2)
                 rsqrt(r, 3)
             else:

@@ -21,12 +21,11 @@ CH = 512
 N_CHUNKS = BATCH * PIX // CH
 AHEAD = 5
 S_ALONE = 3
-S_COLS = 312
-S_COLS_D = 256
-D_FIRST = 1
-D_LAST = 18
-SPREAD = 22
-PAIRS_TO = 0
+S_COLS = 304
+LEAD = 1
+PAIRS_TO = 16
+HALVES_FROM = 20
+FINE_FROM = 22
 PINNED = True
 
 REPARAM = 2.0 ** (-18)
@@ -34,7 +33,7 @@ PEDESTAL = REPARAM * REPARAM
 BETA_BOUND = (1e-06 + PEDESTAL) ** 0.5
 
 PIECES = [(0, 0, 256), (0, 256, 256), (0, 512, 512), (0, 1024, 1024), (0, 2048, 1024), (0, 3072, 1024),
-          (1, 0, 2048), (1, 2048, 2048), (2, 0, 2048), (2, 2048, 2048)]
+          (1, 0, 4096), (2, 0, 4096)]
 
 
 def tile_gdn_t_kernel(tc, inputs, beta, gamma, out):
@@ -138,28 +137,36 @@ def tile_gdn_t_kernel(tc, inputs, beta, gamma, out):
         results = {}
         banks = {}
 
-        def square_a(i, cols):
-            grp = gpool.tile([P, CH, PACK], BF16, name="grp", align_bytes=64)
-            grouped[i] = grp
-            halves[i] = []
-            sc = cols
+        def s_cols(i):
+            return CH if i < S_ALONE else S_COLS
+
+        def group_tile(i):
+            if i not in grouped:
+                grp = gpool.tile([P, CH, PACK], BF16, name="grp", align_bytes=64)
+                grouped[i] = grp
+            return grouped[i]
+
+        def square_s(i):
+            grp = group_tile(i)
             for c0, n, xs in x_parts(i):
-                ns = max(0, min(n, sc - c0))
+                ns = max(0, min(n, s_cols(i) - c0))
                 if ns > 0:
                     nc.scalar.activation(
                         out=grp[:, c0:c0 + ns, :].rearrange("p (c i) t -> p c t i", i=4),
                         in_=xs[:, :, 0:ns].rearrange("p t (c i) -> p c t i", i=4),
                         func=ACT.Square)
-                if ns < n:
-                    sq = spool.tile([P, PACK, n - ns], BF16, name="sq")
-                    nc.vector.tensor_tensor(out=sq[:], in0=xs[:, :, ns:n], in1=xs[:, :, ns:n], op=ALU.mult)
-                    halves[i].append((c0 + ns, c0 + n, sq))
 
-        def square_b(i):
-            for lo, hi, sq in halves[i]:
-                nc.vector.tensor_copy(
-                    out=grouped[i][:, lo:hi, :].rearrange("p (c i) t -> p c t i", i=4),
-                    in_=sq[:].rearrange("p t (c i) -> p c t i", i=4))
+        def square_v1(i):
+            c0, n, xs = x_parts(i)[0]
+            sc = s_cols(i)
+            sq = spool.tile([P, PACK, CH - sc], BF16, name="sq")
+            nc.vector.tensor_tensor(out=sq[:], in0=xs[:, :, sc:CH], in1=xs[:, :, sc:CH], op=ALU.mult)
+            halves[i] = sq
+
+        def square_v2(i):
+            nc.vector.tensor_copy(
+                out=group_tile(i)[:, s_cols(i):CH, :].rearrange("p (c i) t -> p c t i", i=4),
+                in_=halves[i][:].rearrange("p t (c i) -> p c t i", i=4))
 
         def quantise(i):
             codes = cpool.tile([P, CH], U32, name="codes", align_bytes=64)
@@ -207,27 +214,7 @@ def tile_gdn_t_kernel(tc, inputs, beta, gamma, out):
             elif i % 2 == 1:
                 store(i - 1, i + 1, 0, PACK)
 
-        x_banks = {}
-
-        def shared(i):
-            return D_FIRST <= i <= D_LAST
-
-        def x_to_psum(i, j):
-            c0, n, xs = x_parts(i)[0]
-            xp = psum.tile([P, CH], F32, name="xp", tag="acc")
-            nc.tensor.matmul(out=xp[:], lhsT=ident[:], rhs=xs[:, j, :], start=True, stop=True)
-            x_banks[(i, j)] = xp
-
-        def scale_from_psum(i, j):
-            rs = res_view(i)[:, j, :]
-            nc.vector.tensor_tensor(out=rs, in0=x_banks[(i, j)][:], in1=rs, op=ALU.mult)
-
-        def scale_on_gpsimd(i, j):
-            c0, n, xs = x_parts(i)[0]
-            rs = res_view(i)[:, j, :]
-            nc.gpsimd.tensor_tensor(out=rs, in0=xs[:, j, :], in1=rs, op=ALU.mult)
-
-        square_a(0, CH)
+        square_s(0)
         gamma_to_psum()
         beta_step(0)
         quantise(0)
@@ -235,53 +222,47 @@ def tile_gdn_t_kernel(tc, inputs, beta, gamma, out):
         gamma_out(0)
         beta_step(2)
         gamma_out(1)
-        square_a(1, CH)
-        square_a(2, CH)
+        square_s(1)
+        square_s(2)
         quantise(1)
         gamma_quantise()
-        for i in range(3, AHEAD):
-            square_a(i, S_COLS)
-            quantise(i - 1)
-            square_b(i)
-        squared = AHEAD
+        square_v1(3)
+        quantise(2)
+        square_v2(3)
+
+        def front(a):
+            square_s(a)
+            if a + 1 < N_CHUNKS:
+                square_v1(a + 1)
+            quantise(a)
+            if a + 1 < N_CHUNKS:
+                square_v2(a + 1)
+
+        for a in range(3, AHEAD):
+            front(a)
+        nxt = AHEAD
         for r in range(N_CHUNKS):
             c = r - 1
             multiply(r)
-            if shared(r):
-                x_to_psum(r, 0)
-                x_to_psum(r, 3)
-            if c >= 0:
-                if shared(c):
-                    scale_x(c, 2, 3)
+            if 0 <= c < FINE_FROM:
+                scale_x(c, 2, PACK)
+                if c >= HALVES_FROM:
+                    store(c, c + 1, 2, PACK)
                 else:
-                    scale_x(c, 2, PACK)
                     store_chunk(c)
-            want = min(N_CHUNKS, AHEAD + ((r + 1) * (N_CHUNKS - AHEAD) + SPREAD - 1) // SPREAD)
-            fresh = squared < want
-            if fresh:
-                square_a(squared, S_COLS_D if shared(r) else S_COLS)
-            if (squared - 1) not in quantised:
-                quantise(squared - 1)
-            if fresh:
-                square_b(squared)
-                squared += 1
-            if r < N_CHUNKS - 1:
+            if nxt < N_CHUNKS and nxt <= r + LEAD:
+                front(nxt)
+                nxt += 1
+            if r < FINE_FROM:
                 rsqrt(r, 0)
-                if c >= 0 and shared(c):
-                    scale_from_psum(c, 3)
-                    store_chunk(c)
-                if shared(r):
-                    scale_from_psum(r, 0)
-                    rsqrt(r, 1)
-                    scale_on_gpsimd(r, 1)
-                else:
-                    rsqrt(r, 1)
-                    scale_x(r, 0, 2)
+                rsqrt(r, 1)
+                scale_x(r, 0, 2)
+                if r >= HALVES_FROM:
+                    store(r, r + 1, 0, 2)
                 rsqrt(r, 2)
                 rsqrt(r, 3)
             else:
                 for j in range(PACK):
                     rsqrt(r, j)
                     scale_x(r, j, j + 1)
-                    if j >= 1:
-                        store(r, r + 1, 0 if j == 1 else j, j + 1)
+                    store(r, r + 1, j, j + 1)

@@ -22,9 +22,13 @@ N_CHUNKS = BATCH * PIX // CH
 AHEAD = 5
 S_ALONE = 3
 S_COLS = 304
+S_COLS_D = 272
+D_FIRST = 3
+D_LAST = 20
+G_COLS = 384
 LEAD = 1
-PAIRS_TO = 16
-HALVES_FROM = 20
+PAIRS_TO = 0
+HALVES_FROM = 21
 FINE_FROM = 22
 PINNED = True
 
@@ -137,8 +141,13 @@ def tile_gdn_t_kernel(tc, inputs, beta, gamma, out):
         results = {}
         banks = {}
 
+        def shared(i):
+            return D_FIRST <= i <= D_LAST
+
         def s_cols(i):
-            return CH if i < S_ALONE else S_COLS
+            if i < S_ALONE:
+                return CH
+            return S_COLS_D if shared(i - LEAD) else S_COLS
 
         def group_tile(i):
             if i not in grouped:
@@ -238,27 +247,59 @@ def tile_gdn_t_kernel(tc, inputs, beta, gamma, out):
             if a + 1 < N_CHUNKS:
                 square_v2(a + 1)
 
+        x_banks = {}
+
+        def x_to_psum(i, j):
+            c0, n, xs = x_parts(i)[0]
+            xp = psum.tile([P, CH], F32, name="xp", tag="acc")
+            nc.tensor.matmul(out=xp[:], lhsT=ident[:], rhs=xs[:, j, :], start=True, stop=True)
+            x_banks[(i, j)] = xp
+
+        def scale_from_psum(i, j):
+            rs = res_view(i)[:, j, :]
+            nc.vector.tensor_tensor(out=rs, in0=x_banks[(i, j)][:], in1=rs, op=ALU.mult)
+
+        def scale_cols(eng, i, j, lo, hi):
+            c0, n, xs = x_parts(i)[0]
+            rs = res_view(i)[:, j, lo:hi]
+            eng.tensor_tensor(out=rs, in0=xs[:, j, lo:hi], in1=rs, op=ALU.mult)
+
         for a in range(3, AHEAD):
             front(a)
         nxt = AHEAD
         for r in range(N_CHUNKS):
             c = r - 1
             multiply(r)
+            if shared(r):
+                x_to_psum(r, 1)
+                x_to_psum(r, 3)
             if 0 <= c < FINE_FROM:
-                scale_x(c, 2, PACK)
-                if c >= HALVES_FROM:
-                    store(c, c + 1, 2, PACK)
+                if shared(c):
+                    scale_cols(nc.vector, c, 2, 0, CH)
+                    scale_cols(nc.vector, c, 0, G_COLS, CH)
                 else:
-                    store_chunk(c)
+                    scale_x(c, 2, PACK)
+                    if c >= HALVES_FROM:
+                        store(c, c + 1, 2, PACK)
+                    else:
+                        store_chunk(c)
             if nxt < N_CHUNKS and nxt <= r + LEAD:
                 front(nxt)
                 nxt += 1
             if r < FINE_FROM:
                 rsqrt(r, 0)
+                if shared(r):
+                    scale_cols(nc.gpsimd, r, 0, 0, G_COLS)
+                if c >= 0 and shared(c):
+                    scale_from_psum(c, 3)
+                    store_chunk(c)
                 rsqrt(r, 1)
-                scale_x(r, 0, 2)
-                if r >= HALVES_FROM:
-                    store(r, r + 1, 0, 2)
+                if shared(r):
+                    scale_from_psum(r, 1)
+                else:
+                    scale_x(r, 0, 2)
+                    if r >= HALVES_FROM:
+                        store(r, r + 1, 0, 2)
                 rsqrt(r, 2)
                 rsqrt(r, 3)
             else:

@@ -21,8 +21,8 @@ CH = 512
 N_CHUNKS = BATCH * PIX // CH
 AHEAD = 5
 S_ALONE = 3
-S_COLS = 304
-S_COLS_D = 272
+S_COLS = 320
+S_COLS_D = 296
 D_FIRST = 3
 D_LAST = 20
 G_COLS = 384

@@ -27,10 +27,12 @@ D_FIRST = 3
 D_LAST = 20
 G_COLS = 384
 LEAD = 1
-PAIRS_TO = 0
+PAIRS_TO = 20
 HALVES_FROM = 21
 FINE_FROM = 22
 PINNED = True
+LATE_BATCH = 2
+LATE_AFTER = (5, 7, 9, 11)
 
 REPARAM = 2.0 ** (-18)
 PEDESTAL = REPARAM * REPARAM
@@ -68,7 +70,8 @@ def tile_gdn_t_kernel(tc, inputs, beta, gamma, out):
         xt = []
         for n, (b, w0, width) in enumerate(PIECES):
             t = xpool.tile([P, PACK, width], BF16, name="x%d" % n)
-            nc.sync.dma_start(out=t[:], in_=x_dram[b, :, :, w0:w0 + width])
+            if b < LATE_BATCH:
+                nc.sync.dma_start(out=t[:], in_=x_dram[b, :, :, w0:w0 + width])
             xt.append(t)
             if n == 0:
                 nc.sync.dma_start(out=g_raw[:], in_=gamma.rearrange("(m j) c -> m j c", j=PACK))
@@ -222,6 +225,9 @@ def tile_gdn_t_kernel(tc, inputs, beta, gamma, out):
                 store(i, i + 1, 0, PACK)
             elif i % 2 == 1:
                 store(i - 1, i + 1, 0, PACK)
+            if i in LATE_AFTER:
+                j = LATE_AFTER.index(i)
+                nc.sync.dma_start(out=xt[len(PIECES) - 1][:, j, :], in_=x_dram[LATE_BATCH, :, j, :])
 
         square_s(0)
         gamma_to_psum()

@@ -22,17 +22,15 @@ N_CHUNKS = BATCH * PIX // CH
 AHEAD = 5
 S_ALONE = 3
 S_COLS = 320
-S_COLS_D = 296
-D_FIRST = 3
-D_LAST = 20
-G_COLS = 384
+S_COLS_D = 288
+D_FIRST = 2
+D_LAST = 19
+G_COLS = 448
 LEAD = 1
-PAIRS_TO = 20
-HALVES_FROM = 21
+PAIRS_TO = 0
+HALVES_FROM = 20
 FINE_FROM = 22
 PINNED = True
-LATE_BATCH = 2
-LATE_AFTER = (5, 7, 9, 11)
 
 REPARAM = 2.0 ** (-18)
 PEDESTAL = REPARAM * REPARAM
@@ -70,8 +68,7 @@ def tile_gdn_t_kernel(tc, inputs, beta, gamma, out):
         xt = []
         for n, (b, w0, width) in enumerate(PIECES):
             t = xpool.tile([P, PACK, width], BF16, name="x%d" % n)
-            if b < LATE_BATCH:
-                nc.sync.dma_start(out=t[:], in_=x_dram[b, :, :, w0:w0 + width])
+            nc.sync.dma_start(out=t[:], in_=x_dram[b, :, :, w0:w0 + width])
             xt.append(t)
             if n == 0:
                 nc.sync.dma_start(out=g_raw[:], in_=gamma.rearrange("(m j) c -> m j c", j=PACK))
@@ -225,9 +222,6 @@ def tile_gdn_t_kernel(tc, inputs, beta, gamma, out):
                 store(i, i + 1, 0, PACK)
             elif i % 2 == 1:
                 store(i - 1, i + 1, 0, PACK)
-            if i in LATE_AFTER:
-                j = LATE_AFTER.index(i)
-                nc.sync.dma_start(out=xt[len(PIECES) - 1][:, j, :], in_=x_dram[LATE_BATCH, :, j, :])
 
         square_s(0)
         gamma_to_psum()

@@ -19,18 +19,14 @@ BATCH = 3
 PIX = 4096
 CH = 512
 N_CHUNKS = BATCH * PIX // CH
+LAST = N_CHUNKS - 1
 AHEAD = 5
 S_ALONE = 3
 S_COLS = 320
-S_COLS_D = 288
-D_FIRST = 2
-D_LAST = 19
-G_COLS = 448
-LEAD = 1
-PAIRS_TO = 0
-HALVES_FROM = 20
-FINE_FROM = 22
-PINNED = True
+XPX = 256
+V_EXTRA = 0
+G_TWO = 200
+G_ONE = 96
 
 REPARAM = 2.0 ** (-18)
 PEDESTAL = REPARAM * REPARAM
@@ -51,10 +47,10 @@ def tile_gdn_t_kernel(tc, inputs, beta, gamma, out):
         gpool = ctx.enter_context(tc.tile_pool(name="gpool", bufs=4))
         spool = ctx.enter_context(tc.tile_pool(name="spool", bufs=2))
         cpool = ctx.enter_context(tc.tile_pool(name="cpool", bufs=AHEAD + 3))
-        rpool = ctx.enter_context(tc.tile_pool(name="rpool", bufs=4))
-        psum = ctx.enter_context(tc.psum_pool(name="psum", bufs=8))
-        if PINNED:
-            ctx.enter_context(tc.manual_schedule())
+        rpool = ctx.enter_context(tc.tile_pool(name="rpool", bufs=8))
+        psum = ctx.enter_context(tc.psum_pool(name="psum", bufs=4))
+        psumx = ctx.enter_context(tc.psum_pool(name="psumx", bufs=4))
+        ctx.enter_context(tc.manual_schedule())
 
         warm = const.tile([P, 1], F32, name="warm")
         nc.vector.memset(warm[:], 1.0)
@@ -75,15 +71,20 @@ def tile_gdn_t_kernel(tc, inputs, beta, gamma, out):
             if n == 2:
                 nc.sync.dma_start(out=b_raw[:], in_=beta.rearrange("(p j) -> p j", j=PACK))
 
-        def x_parts(i):
+        def x_parts(i, lo=0, hi=CH):
             b, w0 = divmod(i * CH, PIX)
             parts = []
             for k, (pb, pw, width) in enumerate(PIECES):
-                lo = max(pw, w0)
-                hi = min(pw + width, w0 + CH)
-                if pb == b and lo < hi:
-                    parts.append((lo - w0, hi - lo, xt[k][:, :, lo - pw:hi - pw]))
+                a = max(pw, w0 + lo)
+                e = min(pw + width, w0 + hi)
+                if pb == b and a < e:
+                    parts.append((a - w0, e - a, xt[k][:, :, a - pw:e - pw]))
             return parts
+
+        def x_view(i, lo, hi):
+            parts = x_parts(i, lo, hi)
+            assert len(parts) == 1
+            return parts[0][2]
 
         g_codes = const.tile([P, 512], U32, name="g_codes", align_bytes=64)
         g_scales = const.tile([P, 512], U8, name="g_scales", align_bytes=64)
@@ -92,6 +93,8 @@ def tile_gdn_t_kernel(tc, inputs, beta, gamma, out):
 
         b_t = const.tile([P, PACK], F32, name="b_t")
         g_grp = const.tile([P, 512, PACK], BF16, name="g_grp", align_bytes=64)
+        tok_u = const.tile([P, 1], U32, name="tok_u")
+        tok_f = const.tile([P, 1], F32, name="tok_f")
 
         def gamma_to_psum():
             g_u = const.tile([P, PACK, 512], F32, name="g_u")
@@ -140,14 +143,16 @@ def tile_gdn_t_kernel(tc, inputs, beta, gamma, out):
         quantised = {}
         results = {}
         banks = {}
+        x_banks = {}
 
-        def shared(i):
-            return D_FIRST <= i <= D_LAST
+        def in_psum(i):
+            return AHEAD <= i <= LAST
+
+        def s_first(i):
+            return XPX + V_EXTRA
 
         def s_cols(i):
-            if i < S_ALONE:
-                return CH
-            return S_COLS_D if shared(i - LEAD) else S_COLS
+            return CH if i < S_ALONE else S_COLS
 
         def group_tile(i):
             if i not in grouped:
@@ -157,25 +162,36 @@ def tile_gdn_t_kernel(tc, inputs, beta, gamma, out):
 
         def square_s(i):
             grp = group_tile(i)
-            for c0, n, xs in x_parts(i):
-                ns = max(0, min(n, s_cols(i) - c0))
-                if ns > 0:
-                    nc.scalar.activation(
-                        out=grp[:, c0:c0 + ns, :].rearrange("p (c i) t -> p c t i", i=4),
-                        in_=xs[:, :, 0:ns].rearrange("p t (c i) -> p c t i", i=4),
-                        func=ACT.Square)
+            lo, hi = (s_first(i), CH) if in_psum(i) else (0, s_cols(i))
+            for c0, n, xs in x_parts(i, lo, hi):
+                nc.scalar.activation(
+                    out=grp[:, c0:c0 + n, :].rearrange("p (c i) t -> p c t i", i=4),
+                    in_=xs.rearrange("p t (c i) -> p c t i", i=4),
+                    func=ACT.Square)
 
-        def square_v1(i):
-            c0, n, xs = x_parts(i)[0]
-            sc = s_cols(i)
-            sq = spool.tile([P, PACK, CH - sc], BF16, name="sq")
-            nc.vector.tensor_tensor(out=sq[:], in0=xs[:, :, sc:CH], in1=xs[:, :, sc:CH], op=ALU.mult)
+        def square_v1(i, lo, hi):
+            xs = x_view(i, lo, hi)
+            sq = spool.tile([P, PACK, hi - lo], BF16, name="sq")
+            nc.vector.tensor_tensor(out=sq[:], in0=xs, in1=xs, op=ALU.mult)
             halves[i] = sq
 
-        def square_v2(i):
+        def square_v2(i, lo, hi):
             nc.vector.tensor_copy(
-                out=group_tile(i)[:, s_cols(i):CH, :].rearrange("p (c i) t -> p c t i", i=4),
+                out=group_tile(i)[:, lo:hi, :].rearrange("p (c i) t -> p c t i", i=4),
                 in_=halves[i][:].rearrange("p t (c i) -> p c t i", i=4))
+
+        def x_to_psum(i):
+            xb = psumx.tile([P, PACK, XPX], BF16, name="xb")
+            xs = x_view(i, 0, XPX)
+            for t in range(PACK):
+                nc.tensor.matmul(out=xb[:, t, :], lhsT=ident[:], rhs=xs[:, t, :], start=True, stop=True)
+            x_banks[i] = xb
+
+        def square_from_psum(i):
+            nc.vector.tensor_tensor(
+                out=group_tile(i)[:, 0:XPX, :],
+                in0=x_banks[i][:].rearrange("p t w -> p w t"),
+                in1=x_view(i, 0, XPX).rearrange("p t w -> p w t"), op=ALU.mult)
 
         def quantise(i):
             codes = cpool.tile([P, CH], U32, name="codes", align_bytes=64)
@@ -184,44 +200,35 @@ def tile_gdn_t_kernel(tc, inputs, beta, gamma, out):
                                   in_=grouped[i][:].rearrange("p w t -> p (w t)"))
             quantised[i] = (codes, scales)
 
-        def multiply(i):
+        def multiply(i, j):
             codes, scales = quantised[i]
-            for j in range(PACK):
-                acc = psum.tile([P, CH], F32, name="acc", tag="acc")
-                nc.tensor.matmul_mx(out=acc[:],
-                                    lhsT=g_codes[:, P * j:P * j + P].bitcast(FP8X4),
-                                    lhsT_scale=g_scales[:, P * j:P * j + P],
-                                    rhs=codes[:].bitcast(FP8X4), rhs_scale=scales[:],
-                                    start=True, stop=True)
-                banks[(i, j)] = acc
-
-        def res_view(i):
-            return results[i // 2][:, :, (i % 2) * CH:(i % 2 + 1) * CH]
+            acc = psum.tile([P, CH], F32, name="acc", tag="acc")
+            nc.tensor.matmul_mx(out=acc[:],
+                                lhsT=g_codes[:, P * j:P * j + P].bitcast(FP8X4),
+                                lhsT_scale=g_scales[:, P * j:P * j + P],
+                                rhs=codes[:].bitcast(FP8X4), rhs_scale=scales[:],
+                                start=True, stop=True)
+            banks[(i, j)] = acc
 
         def rsqrt(i, j):
-            if i % 2 == 0 and j == 0:
-                res_new = rpool.tile([P, PACK, 2 * CH], F32, name="res")
-                results[i // 2] = res_new
-            nc.scalar.activation(out=res_view(i)[:, j, :], in_=banks[(i, j)][:],
+            if j == 0:
+                res_new = rpool.tile([P, PACK, CH], F32, name="res")
+                results[i] = res_new
+            nc.scalar.activation(out=results[i][:, j, :], in_=banks[(i, j)][:],
                                  func=ACT.Abs_reciprocal_sqrt, bias=b_c[:, j:j + 1], scale=1.0)
 
-        def scale_x(i, j0, j1):
-            for c0, n, xs in x_parts(i):
-                rs = res_view(i)[:, j0:j1, c0:c0 + n]
-                nc.vector.tensor_tensor(out=rs, in0=xs[:, j0:j1, :], in1=rs, op=ALU.mult)
+        def scale_x(eng, i, j0, j1, lo, hi):
+            for c0, n, xs in x_parts(i, lo, hi):
+                rs = results[i][:, j0:j1, c0:c0 + n]
+                eng.tensor_tensor(out=rs, in0=xs[:, j0:j1, :], in1=rs, op=ALU.mult)
 
-        def store(i0, i1, j0, j1):
-            b, w0 = divmod(i0 * CH, PIX)
-            n = (i1 - i0) * CH
-            k0 = (i0 % 2) * CH
-            nc.sync.dma_start(out=o_dram[b, :, j0:j1, w0:w0 + n],
-                              in_=results[i0 // 2][:, j0:j1, k0:k0 + n])
+        def scale_from_psum(i):
+            rs = results[i][:, :, 0:XPX]
+            nc.vector.tensor_tensor(out=rs, in0=x_banks[i][:], in1=rs, op=ALU.mult)
 
-        def store_chunk(i):
-            if i >= PAIRS_TO:
-                store(i, i + 1, 0, PACK)
-            elif i % 2 == 1:
-                store(i - 1, i + 1, 0, PACK)
+        def store(i, j0, j1):
+            b, w0 = divmod(i * CH, PIX)
+            nc.sync.dma_start(out=o_dram[b, :, j0:j1, w0:w0 + CH], in_=results[i][:, j0:j1, :])
 
         square_s(0)
         gamma_to_psum()
@@ -235,75 +242,61 @@ def tile_gdn_t_kernel(tc, inputs, beta, gamma, out):
         square_s(2)
         quantise(1)
         gamma_quantise()
-        square_v1(3)
+        square_v1(3, S_COLS, CH)
         quantise(2)
-        square_v2(3)
+        square_v2(3, S_COLS, CH)
+        square_s(3)
+        square_v1(4, S_COLS, CH)
+        quantise(3)
+        square_v2(4, S_COLS, CH)
+        square_s(4)
+        quantise(4)
+        for j in range(PACK):
+            multiply(0, j)
 
-        def front(a):
-            square_s(a)
-            if a + 1 < N_CHUNKS:
-                square_v1(a + 1)
-            quantise(a)
-            if a + 1 < N_CHUNKS:
-                square_v2(a + 1)
+        def g_pixels(c, a):
+            windows = (1 if in_psum(c) else 0) + (1 if in_psum(a) else 0)
+            if c < 1:
+                return 0
+            return (0, G_ONE, G_TWO)[windows]
 
-        x_banks = {}
-
-        def x_to_psum(i, j):
-            c0, n, xs = x_parts(i)[0]
-            xp = psum.tile([P, CH], F32, name="xp", tag="acc")
-            nc.tensor.matmul(out=xp[:], lhsT=ident[:], rhs=xs[:, j, :], start=True, stop=True)
-            x_banks[(i, j)] = xp
-
-        def scale_from_psum(i, j):
-            rs = res_view(i)[:, j, :]
-            nc.vector.tensor_tensor(out=rs, in0=x_banks[(i, j)][:], in1=rs, op=ALU.mult)
-
-        def scale_cols(eng, i, j, lo, hi):
-            c0, n, xs = x_parts(i)[0]
-            rs = res_view(i)[:, j, lo:hi]
-            eng.tensor_tensor(out=rs, in0=xs[:, j, lo:hi], in1=rs, op=ALU.mult)
-
-        for a in range(3, AHEAD):
-            front(a)
-        nxt = AHEAD
         for r in range(N_CHUNKS):
             c = r - 1
-            multiply(r)
-            if shared(r):
-                x_to_psum(r, 1)
-                x_to_psum(r, 3)
-            if 0 <= c < FINE_FROM:
-                if shared(c):
-                    scale_cols(nc.vector, c, 2, 0, CH)
-                    scale_cols(nc.vector, c, 0, G_COLS, CH)
-                else:
-                    scale_x(c, 2, PACK)
-                    if c >= HALVES_FROM:
-                        store(c, c + 1, 2, PACK)
-                    else:
-                        store_chunk(c)
-            if nxt < N_CHUNKS and nxt <= r + LEAD:
-                front(nxt)
-                nxt += 1
-            if r < FINE_FROM:
-                rsqrt(r, 0)
-                if shared(r):
-                    scale_cols(nc.gpsimd, r, 0, 0, G_COLS)
-                if c >= 0 and shared(c):
-                    scale_from_psum(c, 3)
-                    store_chunk(c)
-                rsqrt(r, 1)
-                if shared(r):
-                    scale_from_psum(r, 1)
-                else:
-                    scale_x(r, 0, 2)
-                    if r >= HALVES_FROM:
-                        store(r, r + 1, 0, 2)
-                rsqrt(r, 2)
-                rsqrt(r, 3)
-            else:
-                for j in range(PACK):
-                    rsqrt(r, j)
-                    scale_x(r, j, j + 1)
-                    store(r, r + 1, j, j + 1)
+            a = r + 2
+            q = r + 1
+            if in_psum(a):
+                square_s(a)
+            token = None
+            if c >= 0:
+                first = XPX if in_psum(c) else 0
+                gp = g_pixels(c, a)
+                if first + gp < CH:
+                    scale_x(nc.vector, c, 0, PACK, first + gp, CH)
+                    token = (tok_f, results[c][:, 0, CH - 1:CH])
+            if in_psum(a) and V_EXTRA > 0:
+                square_v1(a, XPX, XPX + V_EXTRA)
+            if in_psum(q):
+                quantise(q)
+                token = (tok_u, quantised[q][0][:, 0:1])
+            if in_psum(a) and V_EXTRA > 0:
+                square_v2(a, XPX, XPX + V_EXTRA)
+                token = None
+            if c >= 0 and gp > 0:
+                if token is not None:
+                    nc.gpsimd.tensor_copy(out=token[0][:], in_=token[1])
+                scale_x(nc.gpsimd, c, 0, PACK, first, first + gp)
+            if c >= 0 and in_psum(c):
+                scale_from_psum(c)
+            if in_psum(a):
+                square_from_psum(a)
+            if c >= 0:
+                store(c, 0, PACK)
+            for j in range(PACK):
+                rsqrt(r, j)
+                if q <= LAST:
+                    multiply(q, j)
+                if r == LAST:
+                    scale_x(nc.vector, r, j, j + 1, 0, CH)
+                    store(r, j, j + 1)
+            if in_psum(r + 3):
+                x_to_psum(r + 3)

@@ -273,17 +273,20 @@ def tile_gdn_t_kernel(tc, inputs, beta, gamma, out):
                 if first + gp < CH:
                     scale_x(nc.vector, c, 0, PACK, first + gp, CH)
                     token = (tok_f, results[c][:, 0, CH - 1:CH])
+                    if gp > 0:
+                        nc.gpsimd.tensor_copy(out=token[0][:], in_=token[1])
             if in_psum(a) and V_EXTRA > 0:
                 square_v1(a, XPX, XPX + V_EXTRA)
             if in_psum(q):
                 quantise(q)
-                token = (tok_u, quantised[q][0][:, 0:1])
+                if token is None:
+                    token = (tok_u, quantised[q][0][:, 0:1])
+                    if c >= 0 and gp > 0:
+                        nc.gpsimd.tensor_copy(out=token[0][:], in_=token[1])
             if in_psum(a) and V_EXTRA > 0:
                 square_v2(a, XPX, XPX + V_EXTRA)
                 token = None
             if c >= 0 and gp > 0:
-                if token is not None:
-                    nc.gpsimd.tensor_copy(out=token[0][:], in_=token[1])
                 scale_x(nc.gpsimd, c, 0, PACK, first, first + gp)
             if c >= 0 and in_psum(c):
                 scale_from_psum(c)

@@ -165,8 +165,8 @@ def tile_gdn_t_kernel(tc, inputs, beta, gamma, out):
             lo, hi = (s_first(i), CH) if in_psum(i) else (0, s_cols(i))
             for c0, n, xs in x_parts(i, lo, hi):
                 nc.scalar.activation(
-                    out=grp[:, c0:c0 + n, :].rearrange("p (c i) t -> p c t i", i=4),
-                    in_=xs.rearrange("p t (c i) -> p c t i", i=4),
+                    out=grp[:, c0:c0 + n, :].rearrange("p (c i) t -> p c t i", i=8),
+                    in_=xs.rearrange("p t (c i) -> p c t i", i=8),
                     func=ACT.Square)
 
         def square_v1(i, lo, hi):

@@ -22,7 +22,7 @@ N_CHUNKS = BATCH * PIX // CH
 LAST = N_CHUNKS - 1
 AHEAD = 5
 S_ALONE = 3
-S_COLS = 320
+S_COLS = 192
 XPX = 256
 V_EXTRA = 0
 G_TWO = 200
@@ -58,6 +58,8 @@ def tile_gdn_t_kernel(tc, inputs, beta, gamma, out):
 
         ident = const.tile([P, P], BF16, name="ident")
         make_identity(nc, ident[:])
+        ident_f = const.tile([P, P], F32, name="ident_f")
+        make_identity(nc, ident_f[:])
 
         g_raw = const.tile([P, PACK, 512], BF16, name="g_raw")
         b_raw = const.tile([P, PACK], BF16, name="b_raw")
@@ -67,7 +69,9 @@ def tile_gdn_t_kernel(tc, inputs, beta, gamma, out):
             nc.sync.dma_start(out=t[:], in_=x_dram[b, :, :, w0:w0 + width])
             xt.append(t)
             if n == 0:
-                nc.sync.dma_start(out=g_raw[:], in_=gamma.rearrange("(m j) c -> m j c", j=PACK))
+                g_dram = gamma.rearrange("(m j) c -> m j c", j=PACK)
+                nc.sync.dma_start(out=g_raw[:, 0:2, :], in_=g_dram[:, 0:2, :])
+                nc.sync.dma_start(out=g_raw[:, 2:4, :], in_=g_dram[:, 2:4, :])
             if n == 2:
                 nc.sync.dma_start(out=b_raw[:], in_=beta.rearrange("(p j) -> p j", j=PACK))
 
@@ -98,16 +102,15 @@ def tile_gdn_t_kernel(tc, inputs, beta, gamma, out):
 
         def gamma_to_psum():
             g_u = const.tile([P, PACK, 512], F32, name="g_u")
-            g_c = const.tile([P, PACK, PACK, P], BF16, name="g_c")
+            g_c = const.tile([P, PACK, 512], BF16, name="g_c")
 
             def shifted(j):
                 nc.vector.tensor_scalar(out=g_u[:, j, :], in0=g_raw[:, j, :], scalar1=REPARAM,
                                         scalar2=-REPARAM, op0=ALU.max, op1=ALU.add)
 
             def squared_minus(j):
-                u_v = g_u[:, j, :].rearrange("m (p t) -> m t p", t=PACK)
-                nc.vector.scalar_tensor_tensor(out=g_c[:, j, :, :], in0=u_v, scalar=2.0 * REPARAM,
-                                               in1=u_v, op0=ALU.add, op1=ALU.mult)
+                nc.vector.scalar_tensor_tensor(out=g_c[:, j, :], in0=g_u[:, j, :], scalar=2.0 * REPARAM,
+                                               in1=g_u[:, j, :], op0=ALU.add, op1=ALU.mult)
 
             shifted(0)
             for j in range(PACK):
@@ -115,16 +118,18 @@ def tile_gdn_t_kernel(tc, inputs, beta, gamma, out):
                     shifted(j + 1)
                 squared_minus(j)
             for h in range(2):
-                tp = psum.tile([P, 8, P], BF16, name="tp", tag="acc")
+                tp = psum.tile([P, 2, 2, P], F32, name="tp", tag="acc")
                 for jj in range(2):
-                    for t in range(PACK):
-                        nc.tensor.transpose(tp[:, jj * PACK + t, :], g_c[:, 2 * h + jj, t, :], ident[:])
+                    words = g_c[:, 2 * h + jj, :].bitcast(F32)
+                    for u in range(2):
+                        nc.tensor.transpose(tp[:, jj, u, :], words[:, u:256:2], ident_f[:])
                 t_banks.append(tp)
 
         def gamma_out(h):
+            g_words = g_grp[:].rearrange("p w t -> p (w t)").bitcast(F32)
             nc.vector.tensor_copy(
-                out=g_grp[:, 256 * h:256 * h + 256, :].rearrange("p (jj m) t -> p jj m t", jj=2),
-                in_=t_banks[h][:].rearrange("p (jj t) m -> p jj m t", t=PACK))
+                out=g_words[:, 512 * h:512 * h + 512].rearrange("p (jj m u) -> p jj m u", jj=2, u=2),
+                in_=t_banks[h][:].rearrange("p jj u m -> p jj m u"))
 
         def gamma_quantise():
             nc.vector.quantize_mx(out=g_codes[:].bitcast(FP8X4), scales=g_scales[:],
@@ -232,16 +237,16 @@ def tile_gdn_t_kernel(tc, inputs, beta, gamma, out):
 
         square_s(0)
         gamma_to_psum()
-        beta_step(0)
-        quantise(0)
-        beta_step(1)
         gamma_out(0)
-        beta_step(2)
+        quantise(0)
         gamma_out(1)
+        beta_step(0)
+        beta_step(1)
+        beta_step(2)
         square_s(1)
         square_s(2)
-        quantise(1)
         gamma_quantise()
+        quantise(1)
         square_v1(3, S_COLS, CH)
         quantise(2)
         square_v2(3, S_COLS, CH)

from contextlib import ExitStack

import concourse.mybir as mybir
from concourse.masks import make_identity

FLOPS = 2 * 512 * 512 * 3 * 4096

BF16 = mybir.dt.bfloat16
F32 = mybir.dt.float32
U32 = mybir.dt.uint32
U8 = mybir.dt.uint8
FP8X4 = mybir.dt.float8_e4m3fn_x4
ALU = mybir.AluOpType
ACT = mybir.ActivationFunctionType

P = 128
PACK = 4
BATCH = 3
PIX = 4096
CH = 512
N_CHUNKS = BATCH * PIX // CH
LAST = N_CHUNKS - 1
AHEAD = 5
S_ALONE = 3
S_COLS = 192
XPX = 256
V_EXTRA = 0
G_TWO = 200
G_ONE = 96

REPARAM = 2.0 ** (-18)
PEDESTAL = REPARAM * REPARAM
BETA_BOUND = (1e-06 + PEDESTAL) ** 0.5

PIECES = [(0, 0, 256), (0, 256, 256), (0, 512, 512), (0, 1024, 1024), (0, 2048, 1024), (0, 3072, 1024),
          (1, 0, 4096), (2, 0, 4096)]


def tile_gdn_t_kernel(tc, inputs, beta, gamma, out):
    nc = tc.nc
    x_dram = inputs.rearrange("b (p j) h w -> b p j (h w)", j=PACK)
    o_dram = out.rearrange("b (p j) h w -> b p j (h w)", j=PACK)

    with ExitStack() as ctx:
        const = ctx.enter_context(tc.tile_pool(name="const", bufs=1))
        xpool = ctx.enter_context(tc.tile_pool(name="xpool", bufs=1))
        gpool = ctx.enter_context(tc.tile_pool(name="gpool", bufs=4))
        spool = ctx.enter_context(tc.tile_pool(name="spool", bufs=2))
        cpool = ctx.enter_context(tc.tile_pool(name="cpool", bufs=AHEAD + 3))
        rpool = ctx.enter_context(tc.tile_pool(name="rpool", bufs=8))
        psum = ctx.enter_context(tc.psum_pool(name="psum", bufs=4))
        psumx = ctx.enter_context(tc.psum_pool(name="psumx", bufs=4))
        ctx.enter_context(tc.manual_schedule())

        warm = const.tile([P, 1], F32, name="warm")
        nc.vector.memset(warm[:], 1.0)
        nc.scalar.activation(out=warm[:], in_=warm[:], func=ACT.Abs_reciprocal_sqrt)

        ident = const.tile([P, P], BF16, name="ident")
        make_identity(nc, ident[:])
        ident_f = const.tile([P, P], F32, name="ident_f")
        make_identity(nc, ident_f[:])

        g_raw = const.tile([P, PACK, 512], BF16, name="g_raw")
        b_raw = const.tile([P, PACK], BF16, name="b_raw")
        xt = []
        for n, (b, w0, width) in enumerate(PIECES):
            t = xpool.tile([P, PACK, width], BF16, name="x%d" % n)
            nc.sync.dma_start(out=t[:], in_=x_dram[b, :, :, w0:w0 + width])
            xt.append(t)
            if n == 0:
                g_dram = gamma.rearrange("(m j) c -> m j c", j=PACK)
                nc.sync.dma_start(out=g_raw[:, 0:2, :], in_=g_dram[:, 0:2, :])
                nc.sync.dma_start(out=g_raw[:, 2:4, :], in_=g_dram[:, 2:4, :])
            if n == 2:
                nc.sync.dma_start(out=b_raw[:], in_=beta.rearrange("(p j) -> p j", j=PACK))

        def x_parts(i, lo=0, hi=CH):
            b, w0 = divmod(i * CH, PIX)
            parts = []
            for k, (pb, pw, width) in enumerate(PIECES):
                a = max(pw, w0 + lo)
                e = min(pw + width, w0 + hi)
                if pb == b and a < e:
                    parts.append((a - w0, e - a, xt[k][:, :, a - pw:e - pw]))
            return parts

        def x_view(i, lo, hi):
            parts = x_parts(i, lo, hi)
            assert len(parts) == 1
            return parts[0][2]

        g_codes = const.tile([P, 512], U32, name="g_codes", align_bytes=64)
        g_scales = const.tile([P, 512], U8, name="g_scales", align_bytes=64)
        b_c = const.tile([P, PACK], F32, name="b_c")
        t_banks = []

        b_t = const.tile([P, PACK], F32, name="b_t")
        g_grp = const.tile([P, 512, PACK], BF16, name="g_grp", align_bytes=64)
        tok_u = const.tile([P, 1], U32, name="tok_u")
        tok_f = const.tile([P, 1], F32, name="tok_f")

        def gamma_to_psum():
            g_u = const.tile([P, PACK, 512], F32, name="g_u")
            g_c = const.tile([P, PACK, 512], BF16, name="g_c")

            def shifted(j):
                nc.vector.tensor_scalar(out=g_u[:, j, :], in0=g_raw[:, j, :], scalar1=REPARAM,
                                        scalar2=-REPARAM, op0=ALU.max, op1=ALU.add)

            def squared_minus(j):
                nc.vector.scalar_tensor_tensor(out=g_c[:, j, :], in0=g_u[:, j, :], scalar=2.0 * REPARAM,
                                               in1=g_u[:, j, :], op0=ALU.add, op1=ALU.mult)

            shifted(0)
            for j in range(PACK):
                if j + 1 < PACK:
                    shifted(j + 1)
                squared_minus(j)
            for h in range(2):
                tp = psum.tile([P, 2, 2, P], F32, name="tp", tag="acc")
                for jj in range(2):
                    words = g_c[:, 2 * h + jj, :].bitcast(F32)
                    for u in range(2):
                        nc.tensor.transpose(tp[:, jj, u, :], words[:, u:256:2], ident_f[:])
                t_banks.append(tp)

        def gamma_out(h):
            g_words = g_grp[:].rearrange("p w t -> p (w t)").bitcast(F32)
            nc.vector.tensor_copy(
                out=g_words[:, 512 * h:512 * h + 512].rearrange("p (jj m u) -> p jj m u", jj=2, u=2),
                in_=t_banks[h][:].rearrange("p jj u m -> p jj m u"))

        def gamma_quantise():
            nc.vector.quantize_mx(out=g_codes[:].bitcast(FP8X4), scales=g_scales[:],
                                  in_=g_grp[:].rearrange("p w t -> p (w t)"))

        def beta_step(n):
            if n == 0:
                nc.vector.tensor_scalar_max(out=b_t[:], in0=b_raw[:], scalar1=BETA_BOUND)
            elif n == 1:
                nc.vector.tensor_tensor(out=b_t[:], in0=b_t[:], in1=b_t[:], op=ALU.mult)
            else:
                nc.vector.tensor_scalar_add(out=b_c[:], in0=b_t[:], scalar1=-PEDESTAL)

        halves = {}
        grouped = {}
        quantised = {}
        results = {}
        banks = {}
        x_banks = {}

        def in_psum(i):
            return AHEAD <= i <= LAST

        def s_first(i):
            return XPX + V_EXTRA

        def s_cols(i):
            return CH if i < S_ALONE else S_COLS

        def group_tile(i):
            if i not in grouped:
                grp = gpool.tile([P, CH, PACK], BF16, name="grp", align_bytes=64)
                grouped[i] = grp
            return grouped[i]

        def square_s(i):
            grp = group_tile(i)
            lo, hi = (s_first(i), CH) if in_psum(i) else (0, s_cols(i))
            for c0, n, xs in x_parts(i, lo, hi):
                nc.scalar.activation(
                    out=grp[:, c0:c0 + n, :].rearrange("p (c i) t -> p c t i", i=8),
                    in_=xs.rearrange("p t (c i) -> p c t i", i=8),
                    func=ACT.Square)

        def square_v1(i, lo, hi):
            xs = x_view(i, lo, hi)
            sq = spool.tile([P, PACK, hi - lo], BF16, name="sq")
            nc.vector.tensor_tensor(out=sq[:], in0=xs, in1=xs, op=ALU.mult)
            halves[i] = sq

        def square_v2(i, lo, hi):
            nc.vector.tensor_copy(
                out=group_tile(i)[:, lo:hi, :].rearrange("p (c i) t -> p c t i", i=4),
                in_=halves[i][:].rearrange("p t (c i) -> p c t i", i=4))

        def x_to_psum(i):
            xb = psumx.tile([P, PACK, XPX], BF16, name="xb")
            xs = x_view(i, 0, XPX)
            for t in range(PACK):
                nc.tensor.matmul(out=xb[:, t, :], lhsT=ident[:], rhs=xs[:, t, :], start=True, stop=True)
            x_banks[i] = xb

        def square_from_psum(i):
            nc.vector.tensor_tensor(
                out=group_tile(i)[:, 0:XPX, :],
                in0=x_banks[i][:].rearrange("p t w -> p w t"),
                in1=x_view(i, 0, XPX).rearrange("p t w -> p w t"), op=ALU.mult)

        def quantise(i):
            codes = cpool.tile([P, CH], U32, name="codes", align_bytes=64)
            scales = cpool.tile([P, CH], U8, name="scales", align_bytes=64)
            nc.vector.quantize_mx(out=codes[:].bitcast(FP8X4), scales=scales[:],
                                  in_=grouped[i][:].rearrange("p w t -> p (w t)"))
            quantised[i] = (codes, scales)

        def multiply(i, j):
            codes, scales = quantised[i]
            acc = psum.tile([P, CH], F32, name="acc", tag="acc")
            nc.tensor.matmul_mx(out=acc[:],
                                lhsT=g_codes[:, P * j:P * j + P].bitcast(FP8X4),
                                lhsT_scale=g_scales[:, P * j:P * j + P],
                                rhs=codes[:].bitcast(FP8X4), rhs_scale=scales[:],
                                start=True, stop=True)
            banks[(i, j)] = acc

        def rsqrt(i, j):
            if j == 0:
                res_new = rpool.tile([P, PACK, CH], F32, name="res")
                results[i] = res_new
            nc.scalar.activation(out=results[i][:, j, :], in_=banks[(i, j)][:],
                                 func=ACT.Abs_reciprocal_sqrt, bias=b_c[:, j:j + 1], scale=1.0)

        def scale_x(eng, i, j0, j1, lo, hi):
            for c0, n, xs in x_parts(i, lo, hi):
                rs = results[i][:, j0:j1, c0:c0 + n]
                eng.tensor_tensor(out=rs, in0=xs[:, j0:j1, :], in1=rs, op=ALU.mult)

        def scale_from_psum(i):
            rs = results[i][:, :, 0:XPX]
            nc.vector.tensor_tensor(out=rs, in0=x_banks[i][:], in1=rs, op=ALU.mult)

        def store(i, j0, j1):
            b, w0 = divmod(i * CH, PIX)
            nc.sync.dma_start(out=o_dram[b, :, j0:j1, w0:w0 + CH], in_=results[i][:, j0:j1, :])

        square_s(0)
        gamma_to_psum()
        gamma_out(0)
        quantise(0)
        gamma_out(1)
        beta_step(0)
        beta_step(1)
        beta_step(2)
        square_s(1)
        square_s(2)
        gamma_quantise()
        quantise(1)
        square_v1(3, S_COLS, CH)
        quantise(2)
        square_v2(3, S_COLS, CH)
        square_s(3)
        square_v1(4, S_COLS, CH)
        quantise(3)
        square_v2(4, S_COLS, CH)
        square_s(4)
        quantise(4)
        for j in range(PACK):
            multiply(0, j)

        def g_pixels(c, a):
            windows = (1 if in_psum(c) else 0) + (1 if in_psum(a) else 0)
            if c < 1:
                return 0
            return (0, G_ONE, G_TWO)[windows]

        for r in range(N_CHUNKS):
            c = r - 1
            a = r + 2
            q = r + 1
            if in_psum(a):
                square_s(a)
            token = None
            if c >= 0:
                first = XPX if in_psum(c) else 0
                gp = g_pixels(c, a)
                if first + gp < CH:
                    scale_x(nc.vector, c, 0, PACK, first + gp, CH)
                    token = (tok_f, results[c][:, 0, CH - 1:CH])
                    if gp > 0:
                        nc.gpsimd.tensor_copy(out=token[0][:], in_=token[1])
            if in_psum(a) and V_EXTRA > 0:
                square_v1(a, XPX, XPX + V_EXTRA)
            if in_psum(q):
                quantise(q)
                if token is None:
                    token = (tok_u, quantised[q][0][:, 0:1])
                    if c >= 0 and gp > 0:
                        nc.gpsimd.tensor_copy(out=token[0][:], in_=token[1])
            if in_psum(a) and V_EXTRA > 0:
                square_v2(a, XPX, XPX + V_EXTRA)
                token = None
            if c >= 0 and gp > 0:
                scale_x(nc.gpsimd, c, 0, PACK, first, first + gp)
            if c >= 0 and in_psum(c):
                scale_from_psum(c)
            if in_psum(a):
                square_from_psum(a)
            if c >= 0:
                store(c, 0, PACK)
            for j in range(PACK):
                rsqrt(r, j)
                if q <= LAST:
                    multiply(q, j)
                if r == LAST:
                    scale_x(nc.vector, r, j, j + 1, 0, CH)
                    store(r, j, j + 1)
            if in_psum(r + 3):
                x_to_psum(r + 3)
